import numpy as np
import ml_dtypes

BF16 = ml_dtypes.bfloat16


def bf(x):
    return np.asarray(x, np.float32).astype(BF16)


def f32(x):
    return np.asarray(x, np.float32)


def f64(x):
    return np.asarray(x).astype(np.float64)


def striped(idx):
    return np.tile(idx.reshape(-1, 16).T, (8, 1))


C, KVH, D, S, N = 256, 2, 128, 512, 64
ZP, LO, HI = 8.0, 1, 16


def setup_inputs():
    nib = np.random.choice(np.arange(LO, HI), size=(KVH, D, N))
    nib[:, 0, :] = HI - 1
    scale = np.repeat(0.3 + 0.2 * np.random.random((KVH, 1, N)), D, axis=1)
    return {"base": f32(np.random.standard_normal((C, S))), "nib": f32(nib.reshape(C, N)), "scale": f32(scale.reshape(C, N)), "offs": striped(np.random.permutation(S)[:N])}


def reference(base, nib, scale, offs):
    idx = offs[:16].T.reshape(-1)
    res = f64(base).copy()
    res[:, idx] = (f64(nib) - ZP) * f64(scale)
    return res

@@ -1,0 +1,39 @@
+import concourse.mybir as mybir
+
+P = 128
+F32 = mybir.dt.float32
+U16 = mybir.dt.uint16
+ZERO_POINT = 8.0
+OFFSETS_PER_COLUMN = 16
+
+
+def tile_eccpagedattentionshim_kernel(tc, base, nib, scale, offs, out):
+    nc = tc.nc
+    channels, slots = base.shape
+    tokens = nib.shape[1]
+    assert channels % P == 0 and tokens % OFFSETS_PER_COLUMN == 0
+
+    with (
+        tc.tile_pool(name="held", bufs=1) as held,
+        tc.tile_pool(name="work", bufs=2) as work,
+    ):
+        offsets = held.tile([P, tokens // OFFSETS_PER_COLUMN], U16, name="offsets")
+        nc.sync.dma_start(offsets[:], offs)
+
+        for block in range(channels // P):
+            rows = slice(block * P, (block + 1) * P)
+
+            cache = work.tile([P, slots], F32)
+            nc.sync.dma_start(cache[:], base[rows, :])
+            codes = work.tile([P, tokens], F32)
+            nc.sync.dma_start(codes[:], nib[rows, :])
+            steps = work.tile([P, tokens], F32)
+            nc.sync.dma_start(steps[:], scale[rows, :])
+
+            centred = work.tile([P, tokens], F32)
+            nc.vector.tensor_scalar_sub(centred[:], codes[:], ZERO_POINT)
+
+            nc.vector.tensor_tensor(
+                cache[:].indirect(offsets[:]), centred[:], steps[:], mybir.AluOpType.mult
+            )
+            nc.sync.dma_start(out[rows, :], cache[:])

@@ -12,28 +12,31 @@ def tile_eccpagedattentionshim_kernel(tc, base, nib, scale, offs, out):
     channels, slots = base.shape
     tokens = nib.shape[1]
     assert channels % P == 0 and tokens % OFFSETS_PER_COLUMN == 0
+    blocks = channels // P
 
-    with (
-        tc.tile_pool(name="held", bufs=1) as held,
-        tc.tile_pool(name="work", bufs=2) as work,
-    ):
+    with tc.tile_pool(name="held", bufs=1) as held:
         offsets = held.tile([P, tokens // OFFSETS_PER_COLUMN], U16, name="offsets")
         nc.sync.dma_start(offsets[:], offs)
 
-        for block in range(channels // P):
-            rows = slice(block * P, (block + 1) * P)
+        caches = []
+        for block in range(blocks):
+            cache = held.tile([P, slots], F32, name=f"cache{block}")
+            nc.sync.dma_start(cache[:], base[block * P : (block + 1) * P, :])
+            caches.append(cache)
 
-            cache = work.tile([P, slots], F32)
-            nc.sync.dma_start(cache[:], base[rows, :])
-            codes = work.tile([P, tokens], F32)
-            nc.sync.dma_start(codes[:], nib[rows, :])
-            steps = work.tile([P, tokens], F32)
-            nc.sync.dma_start(steps[:], scale[rows, :])
+        codes = held.tile([P, blocks, tokens], F32, name="codes")
+        nc.scalar.dma_start(codes[:], nib.rearrange("(b p) n -> p b n", p=P))
+        steps = held.tile([P, blocks, tokens], F32, name="steps")
+        nc.scalar.dma_start(steps[:], scale.rearrange("(b p) n -> p b n", p=P))
 
-            centred = work.tile([P, tokens], F32)
-            nc.vector.tensor_scalar_sub(centred[:], codes[:], ZERO_POINT)
+        centred = held.tile([P, blocks, tokens], F32, name="centred")
+        nc.vector.tensor_scalar_sub(centred[:], codes[:], ZERO_POINT)
 
+        for block in range(blocks):
             nc.vector.tensor_tensor(
-                cache[:].indirect(offsets[:]), centred[:], steps[:], mybir.AluOpType.mult
+                caches[block][:].indirect(offsets[:]),
+                centred[:, block, :],
+                steps[:, block, :],
+                mybir.AluOpType.mult,
             )
-            nc.sync.dma_start(out[rows, :], cache[:])
+            nc.sync.dma_start(out[block * P : (block + 1) * P, :], caches[block][:])

@@ -14,6 +14,9 @@ def tile_eccpagedattentionshim_kernel(tc, base, nib, scale, offs, out):
     assert channels % P == 0 and tokens % OFFSETS_PER_COLUMN == 0
     blocks = channels // P
 
+    base_blocks = base.rearrange("(p b) s -> b p s", b=blocks)
+    out_blocks = out.rearrange("(p b) s -> b p s", b=blocks)
+
     with tc.tile_pool(name="held", bufs=1) as held:
         offsets = held.tile([P, tokens // OFFSETS_PER_COLUMN], U16, name="offsets")
         nc.sync.dma_start(offsets[:], offs)
@@ -21,13 +24,13 @@ def tile_eccpagedattentionshim_kernel(tc, base, nib, scale, offs, out):
         caches = []
         for block in range(blocks):
             cache = held.tile([P, slots], F32, name=f"cache{block}")
-            nc.sync.dma_start(cache[:], base[block * P : (block + 1) * P, :])
+            nc.sync.dma_start(cache[:], base_blocks[block])
             caches.append(cache)
 
         codes = held.tile([P, blocks, tokens], F32, name="codes")
-        nc.scalar.dma_start(codes[:], nib.rearrange("(b p) n -> p b n", p=P))
+        nc.scalar.dma_start(codes[:], nib.rearrange("(p b) n -> p b n", b=blocks))
         steps = held.tile([P, blocks, tokens], F32, name="steps")
-        nc.scalar.dma_start(steps[:], scale.rearrange("(b p) n -> p b n", p=P))
+        nc.scalar.dma_start(steps[:], scale.rearrange("(p b) n -> p b n", b=blocks))
 
         centred = held.tile([P, blocks, tokens], F32, name="centred")
         nc.vector.tensor_scalar_sub(centred[:], codes[:], ZERO_POINT)
@@ -39,4 +42,5 @@ def tile_eccpagedattentionshim_kernel(tc, base, nib, scale, offs, out):
                 steps[:, block, :],
                 mybir.AluOpType.mult,
             )
-            nc.sync.dma_start(out[block * P : (block + 1) * P, :], caches[block][:])
+            store_queue = nc.sync if block % 2 == 0 else nc.scalar
+            store_queue.dma_start(out_blocks[block], caches[block][:])

@@ -42,5 +42,4 @@ def tile_eccpagedattentionshim_kernel(tc, base, nib, scale, offs, out):
                 steps[:, block, :],
                 mybir.AluOpType.mult,
             )
-            store_queue = nc.sync if block % 2 == 0 else nc.scalar
-            store_queue.dma_start(out_blocks[block], caches[block][:])
+            nc.sync.dma_start(out_blocks[block], caches[block][:])

@@ -5,6 +5,7 @@ F32 = mybir.dt.float32
 U16 = mybir.dt.uint16
 ZERO_POINT = 8.0
 OFFSETS_PER_COLUMN = 16
+HEAD_CHANNELS = 128
 
 
 def tile_eccpagedattentionshim_kernel(tc, base, nib, scale, offs, out):
@@ -13,6 +14,7 @@ def tile_eccpagedattentionshim_kernel(tc, base, nib, scale, offs, out):
     tokens = nib.shape[1]
     assert channels % P == 0 and tokens % OFFSETS_PER_COLUMN == 0
     blocks = channels // P
+    assert HEAD_CHANNELS % blocks == 0
 
     base_blocks = base.rearrange("(p b) s -> b p s", b=blocks)
     out_blocks = out.rearrange("(p b) s -> b p s", b=blocks)
@@ -29,8 +31,8 @@ def tile_eccpagedattentionshim_kernel(tc, base, nib, scale, offs, out):
 
         codes = held.tile([P, blocks, tokens], F32, name="codes")
         nc.scalar.dma_start(codes[:], nib.rearrange("(p b) n -> p b n", b=blocks))
-        steps = held.tile([P, blocks, tokens], F32, name="steps")
-        nc.scalar.dma_start(steps[:], scale.rearrange("(p b) n -> p b n", b=blocks))
+        steps = held.tile([P, tokens], F32, name="steps")
+        nc.scalar.dma_start(steps[:], scale.rearrange("(p b) n -> b p n", b=blocks)[0])
 
         centred = held.tile([P, blocks, tokens], F32, name="centred")
         nc.vector.tensor_scalar_sub(centred[:], codes[:], ZERO_POINT)
@@ -39,7 +41,7 @@ def tile_eccpagedattentionshim_kernel(tc, base, nib, scale, offs, out):
             nc.vector.tensor_tensor(
                 caches[block][:].indirect(offsets[:]),
                 centred[:, block, :],
-                steps[:, block, :],
+                steps[:],
                 mybir.AluOpType.mult,
             )
             nc.sync.dma_start(out_blocks[block], caches[block][:])

@@ -22,17 +22,15 @@ def tile_eccpagedattentionshim_kernel(tc, base, nib, scale, offs, out):
     with tc.tile_pool(name="held", bufs=1) as held:
         offsets = held.tile([P, tokens // OFFSETS_PER_COLUMN], U16, name="offsets")
         nc.sync.dma_start(offsets[:], offs)
-
+        codes = held.tile([P, blocks, tokens], F32, name="codes")
+        nc.sync.dma_start(codes[:], nib.rearrange("(p b) n -> p b n", b=blocks))
+        steps = held.tile([P, tokens], F32, name="steps")
+        nc.sync.dma_start(steps[:], scale.rearrange("(p b) n -> b p n", b=blocks)[0])
         caches = []
         for block in range(blocks):
             cache = held.tile([P, slots], F32, name=f"cache{block}")
             nc.sync.dma_start(cache[:], base_blocks[block])
             caches.append(cache)
-
-        codes = held.tile([P, blocks, tokens], F32, name="codes")
-        nc.scalar.dma_start(codes[:], nib.rearrange("(p b) n -> p b n", b=blocks))
-        steps = held.tile([P, tokens], F32, name="steps")
-        nc.scalar.dma_start(steps[:], scale.rearrange("(p b) n -> b p n", b=blocks)[0])
 
         centred = held.tile([P, blocks, tokens], F32, name="centred")
         nc.vector.tensor_scalar_sub(centred[:], codes[:], ZERO_POINT)

@@ -22,23 +22,25 @@ def tile_eccpagedattentionshim_kernel(tc, base, nib, scale, offs, out):
     with tc.tile_pool(name="held", bufs=1) as held:
         offsets = held.tile([P, tokens // OFFSETS_PER_COLUMN], U16, name="offsets")
         nc.sync.dma_start(offsets[:], offs)
-        codes = held.tile([P, blocks, tokens], F32, name="codes")
-        nc.sync.dma_start(codes[:], nib.rearrange("(p b) n -> p b n", b=blocks))
         steps = held.tile([P, tokens], F32, name="steps")
         nc.sync.dma_start(steps[:], scale.rearrange("(p b) n -> b p n", b=blocks)[0])
+        nib_blocks = nib.rearrange("(p b) n -> b p n", b=blocks)
+        codes = []
         caches = []
         for block in range(blocks):
+            code = held.tile([P, tokens], F32, name=f"code{block}")
+            nc.sync.dma_start(code[:], nib_blocks[block])
+            codes.append(code)
             cache = held.tile([P, slots], F32, name=f"cache{block}")
             nc.sync.dma_start(cache[:], base_blocks[block])
             caches.append(cache)
 
-        centred = held.tile([P, blocks, tokens], F32, name="centred")
-        nc.vector.tensor_scalar_sub(centred[:], codes[:], ZERO_POINT)
-
         for block in range(blocks):
+            centred = held.tile([P, tokens], F32, name=f"centred{block}")
+            nc.scalar.add(centred[:], codes[block][:], -ZERO_POINT)
             nc.vector.tensor_tensor(
                 caches[block][:].indirect(offsets[:]),
-                centred[:, block, :],
+                centred[:],
                 steps[:],
                 mybir.AluOpType.mult,
             )

@@ -20,17 +20,18 @@ def tile_eccpagedattentionshim_kernel(tc, base, nib, scale, offs, out):
     out_blocks = out.rearrange("(p b) s -> b p s", b=blocks)
 
     with tc.tile_pool(name="held", bufs=1) as held:
-        offsets = held.tile([P, tokens // OFFSETS_PER_COLUMN], U16, name="offsets")
-        nc.sync.dma_start(offsets[:], offs)
-        steps = held.tile([P, tokens], F32, name="steps")
-        nc.sync.dma_start(steps[:], scale.rearrange("(p b) n -> b p n", b=blocks)[0])
         nib_blocks = nib.rearrange("(p b) n -> b p n", b=blocks)
+        offsets = held.tile([P, tokens // OFFSETS_PER_COLUMN], U16, name="offsets")
+        steps = held.tile([P, tokens], F32, name="steps")
         codes = []
         caches = []
         for block in range(blocks):
             code = held.tile([P, tokens], F32, name=f"code{block}")
             nc.sync.dma_start(code[:], nib_blocks[block])
             codes.append(code)
+            if block == 0:
+                nc.sync.dma_start(offsets[:], offs)
+                nc.sync.dma_start(steps[:], scale.rearrange("(p b) n -> b p n", b=blocks)[0])
             cache = held.tile([P, slots], F32, name=f"cache{block}")
             nc.sync.dma_start(cache[:], base_blocks[block])
             caches.append(cache)

@@ -38,7 +38,7 @@ def tile_eccpagedattentionshim_kernel(tc, base, nib, scale, offs, out):
 
         for block in range(blocks):
             centred = held.tile([P, tokens], F32, name=f"centred{block}")
-            nc.scalar.add(centred[:], codes[block][:], -ZERO_POINT)
+            nc.vector.tensor_scalar_sub(centred[:], codes[block][:], ZERO_POINT)
             nc.vector.tensor_tensor(
                 caches[block][:].indirect(offsets[:]),
                 centred[:],

@@ -22,16 +22,17 @@ def tile_eccpagedattentionshim_kernel(tc, base, nib, scale, offs, out):
     with tc.tile_pool(name="held", bufs=1) as held:
         nib_blocks = nib.rearrange("(p b) n -> b p n", b=blocks)
         offsets = held.tile([P, tokens // OFFSETS_PER_COLUMN], U16, name="offsets")
+        nc.sync.dma_start(offsets[:], offs)
         steps = held.tile([P, tokens], F32, name="steps")
         codes = []
         caches = []
         for block in range(blocks):
             code = held.tile([P, tokens], F32, name=f"code{block}")
-            nc.sync.dma_start(code[:], nib_blocks[block])
+            code_queue = nc.scalar if block == 0 else nc.sync
+            code_queue.dma_start(code[:], nib_blocks[block])
             codes.append(code)
             if block == 0:
-                nc.sync.dma_start(offsets[:], offs)
-                nc.sync.dma_start(steps[:], scale.rearrange("(p b) n -> b p n", b=blocks)[0])
+                nc.scalar.dma_start(steps[:], scale.rearrange("(p b) n -> b p n", b=blocks)[0])
             cache = held.tile([P, slots], F32, name=f"cache{block}")
             nc.sync.dma_start(cache[:], base_blocks[block])
             caches.append(cache)

@@ -25,7 +25,6 @@ def tile_eccpagedattentionshim_kernel(tc, base, nib, scale, offs, out):
         nc.sync.dma_start(offsets[:], offs)
         steps = held.tile([P, tokens], F32, name="steps")
         codes = []
-        caches = []
         for block in range(blocks):
             code = held.tile([P, tokens], F32, name=f"code{block}")
             code_queue = nc.scalar if block == 0 else nc.sync
@@ -33,16 +32,22 @@ def tile_eccpagedattentionshim_kernel(tc, base, nib, scale, offs, out):
             codes.append(code)
             if block == 0:
                 nc.scalar.dma_start(steps[:], scale.rearrange("(p b) n -> b p n", b=blocks)[0])
+        caches = []
+        for block in range(blocks):
             cache = held.tile([P, slots], F32, name=f"cache{block}")
             nc.sync.dma_start(cache[:], base_blocks[block])
             caches.append(cache)
 
+        centred = []
         for block in range(blocks):
-            centred = held.tile([P, tokens], F32, name=f"centred{block}")
-            nc.vector.tensor_scalar_sub(centred[:], codes[block][:], ZERO_POINT)
+            centred_code = held.tile([P, tokens], F32, name=f"centred{block}")
+            nc.vector.tensor_scalar_sub(centred_code[:], codes[block][:], ZERO_POINT)
+            centred.append(centred_code)
+
+        for block in range(blocks):
             nc.vector.tensor_tensor(
                 caches[block][:].indirect(offsets[:]),
-                centred[:],
+                centred[block][:],
                 steps[:],
                 mybir.AluOpType.mult,
             )

import concourse.mybir as mybir

P = 128
F32 = mybir.dt.float32
U16 = mybir.dt.uint16
ZERO_POINT = 8.0
OFFSETS_PER_COLUMN = 16
HEAD_CHANNELS = 128


def tile_eccpagedattentionshim_kernel(tc, base, nib, scale, offs, out):
    nc = tc.nc
    channels, slots = base.shape
    tokens = nib.shape[1]
    assert channels % P == 0 and tokens % OFFSETS_PER_COLUMN == 0
    blocks = channels // P
    assert HEAD_CHANNELS % blocks == 0

    base_blocks = base.rearrange("(p b) s -> b p s", b=blocks)
    out_blocks = out.rearrange("(p b) s -> b p s", b=blocks)

    with tc.tile_pool(name="held", bufs=1) as held:
        nib_blocks = nib.rearrange("(p b) n -> b p n", b=blocks)
        offsets = held.tile([P, tokens // OFFSETS_PER_COLUMN], U16, name="offsets")
        nc.sync.dma_start(offsets[:], offs)
        steps = held.tile([P, tokens], F32, name="steps")
        codes = []
        for block in range(blocks):
            code = held.tile([P, tokens], F32, name=f"code{block}")
            code_queue = nc.scalar if block == 0 else nc.sync
            code_queue.dma_start(code[:], nib_blocks[block])
            codes.append(code)
            if block == 0:
                nc.scalar.dma_start(steps[:], scale.rearrange("(p b) n -> b p n", b=blocks)[0])
        caches = []
        for block in range(blocks):
            cache = held.tile([P, slots], F32, name=f"cache{block}")
            nc.sync.dma_start(cache[:], base_blocks[block])
            caches.append(cache)

        centred = []
        for block in range(blocks):
            centred_code = held.tile([P, tokens], F32, name=f"centred{block}")
            nc.vector.tensor_scalar_sub(centred_code[:], codes[block][:], ZERO_POINT)
            centred.append(centred_code)

        for block in range(blocks):
            nc.vector.tensor_tensor(
                caches[block][:].indirect(offsets[:]),
                centred[block][:],
                steps[:],
                mybir.AluOpType.mult,
            )
            nc.sync.dma_start(out_blocks[block], caches[block][:])
